import numpy as np
import ml_dtypes


BF16 = ml_dtypes.bfloat16


def bf(x):
    return np.asarray(x, np.float32).astype(BF16)


def f64(x):
    return np.asarray(x).astype(np.float64)


E2M1 = np.array([0.0, 0.5, 1.0, 1.5, 2.0, 3.0, 4.0, 6.0, -0.0, -0.5, -1.0, -1.5, -2.0, -3.0, -4.0, -6.0])


def pack_weight(w, fmt):
    k, n = w.shape
    w = f64(bf(w)).reshape(k // 32, 32, n)
    amax = np.abs(w).max(1)
    if fmt == "e4m3":
        byte = np.frexp(amax)[1] - 1 + 127 - 7
    else:
        mant, ex = np.frexp(amax / 6.0)
        byte = np.where(mant > 0.5, ex, ex - 1) + 127
    byte = np.clip(np.where(amax > 0, byte, 1), 1, 254)
    scaled = (w * np.exp2(127.0 - byte)[:, None, :]).reshape(k, n).astype(np.float32)
    by_word = np.ascontiguousarray(scaled.reshape(k // 512, 128, 4, n).transpose(0, 1, 3, 2))
    if fmt == "e4m3":
        words = by_word.astype(ml_dtypes.float8_e4m3fn).view(np.uint8)
    else:
        c = by_word.astype(ml_dtypes.float4_e2m1fn).view(np.uint8) & 0xF
        words = c[..., 0::2] | (c[..., 1::2] << 4)
    return np.ascontiguousarray(words), np.ascontiguousarray(byte.astype(np.uint8).reshape(k // 512, 16, n))


def unpack_weight(words, scales, fmt):
    g, p, n, _ = words.shape
    if fmt == "e4m3":
        vals = np.ascontiguousarray(words).view(ml_dtypes.float8_e4m3fn).astype(np.float64)
    else:
        nib = np.empty((g, p, n, 4), np.uint8)
        nib[..., 0::2] = words & 0xF
        nib[..., 1::2] = words >> 4
        vals = E2M1[nib]
    vals = vals * np.repeat(np.exp2(scales.astype(np.float64) - 127.0), 8, axis=1)[..., None]
    return vals.transpose(0, 1, 3, 2).reshape(g * 512, n)

def pack4(w):
    words, scales = pack_weight(w, "e2m1")
    return words.reshape(words.shape[0], 128, -1), scales


def unpack4(words, scales):
    return unpack_weight(words.reshape(words.shape[0], 128, -1, 2), scales, "e2m1")


def kspread(k):
    return np.exp2(np.repeat(np.random.randint(-6, 7, k // 32), 32).astype(np.float64))


B, S, C, HD = 1, 1024, 4096, 128
H = C // HD
HP = HD // 2
EPS = 1e-6
THETA = 10000.0


def rmsnorm(h, g):
    return h * (1.0 / np.sqrt(np.mean(h * h, axis=-1, keepdims=True) + EPS)) * g


def apply_rope1(h, freqs):
    sh = h.shape
    h_ = h.reshape(*sh[:-1], -1, 1, 2)
    out = freqs[..., 0] * h_[..., 0] + freqs[..., 1] * h_[..., 1]
    return out.reshape(sh)


def setup_inputs():
    s = kspread(C)
    pos = f64(np.random.randint(0, S, size=(S, 1)))
    inv_freq = 1.0 / THETA ** (np.arange(HP) / HP)
    ang = pos * inv_freq
    cos, sin = np.cos(ang), np.sin(ang)
    rot = np.stack([np.stack([cos, -sin], -1), np.stack([sin, cos], -1)], -2)
    x = np.random.standard_normal((B, S, C)) * s
    x_words, x_scales = pack4(np.ascontiguousarray(x.reshape(B * S, C).T))
    w = np.random.standard_normal((C, C)) / np.sqrt(C) / s[None, :]
    w_words, w_scales = pack4(np.ascontiguousarray(w.T))
    return {"x_words": x_words,
            "x_scales": x_scales,
            "freqs": bf(rot[None, :, None]),
            "w_words": w_words,
            "w_scales": w_scales,
            "b": bf(np.random.standard_normal(C) * 0.3),
            "g": bf(1.0 + 0.1 * np.random.standard_normal(HD))}


def reference(x_words, x_scales, freqs, w_words, w_scales, b, g):
    xq = unpack4(x_words, x_scales).T.reshape(B, S, C)
    p = (xq @ unpack4(w_words, w_scales)) + f64(b)
    h = p.reshape(B, S, H, HD)
    return apply_rope1(rmsnorm(h, f64(g)), f64(freqs))

@@ -1,0 +1,241 @@
+from contextlib import ExitStack
+
+import concourse.mybir as mybir
+from concourse.masks import make_identity
+
+F32 = mybir.dt.float32
+BF16 = mybir.dt.bfloat16
+I32 = mybir.dt.int32
+U8 = mybir.dt.uint8
+FP4X4 = mybir.dt.float4_e2m1fn_x4
+ADD = mybir.AluOpType.add
+MULT = mybir.AluOpType.mult
+ACT = mybir.ActivationFunctionType
+
+P = 128
+TOKENS = 1024
+C = 4096
+GROUPS = C // 512
+HD = 128
+HEADS = C // HD
+PAIRS = HD // 2
+EPS = 1e-6
+BLOCK = 512
+HEADS_BLOCK = BLOCK // HD
+TILES = TOKENS // P
+HALF_T = TILES // 2
+HALF_TOK = HALF_T * P
+
+FLOPS = 2 * TOKENS * C * C
+
+W_RANGES = [(0, 512), (512, 512), (1024, 1024), (2048, 1024), (3072, 1024)]
+
+CHUNKS = (
+    [(0, 0, 2), (0, 2, 2), (0, 4, 4)]
+    + [(blk, t0, 4) for blk in range(1, 7) for t0 in (0, 4)]
+    + [(7, 0, 4), (7, 4, 2), (7, 6, 1), (7, 7, 1)]
+)
+
+
+def tile_selfattention_pa_kernel(tc, x_words, x_scales, freqs, w_words, w_scales, b, g, out):
+    nc = tc.nc
+    out_v = out.rearrange("a (t p) h d -> p (a t) (h d)", p=P)
+    freqs_v = freqs.rearrange("a (t p) c j i k -> p (a t) (c j i k)", p=P)
+
+    with ExitStack() as ctx:
+        keep = ctx.enter_context(tc.tile_pool(name="keep", bufs=1))
+        work = ctx.enter_context(tc.tile_pool(name="work", bufs=2))
+        small = ctx.enter_context(tc.tile_pool(name="small", bufs=3))
+        psum = ctx.enter_context(tc.psum_pool(name="psum", bufs=8))
+        ctx.enter_context(tc.manual_schedule())
+
+        xc = [keep.tile([P, GROUPS, 2 * HALF_TOK], U8, name="xc%d" % i, align_bytes=64) for i in range(2)]
+        xs = [keep.tile([P, GROUPS, HALF_TOK], U8, name="xs%d" % i, align_bytes=64) for i in range(2)]
+        wc = [keep.tile([P, GROUPS, 2 * n], U8, name="wc%d" % i, align_bytes=64) for i, (c0, n) in enumerate(W_RANGES)]
+        ws = [keep.tile([P, GROUPS, n], U8, name="ws%d" % i, align_bytes=64) for i, (c0, n) in enumerate(W_RANGES)]
+        bg = keep.tile([P, HD], BF16, name="bg")
+        ident = keep.tile([P, P], BF16, name="ident")
+        bias = keep.tile([P, C // BLOCK, BLOCK], F32, name="bias")
+        gain = keep.tile([P, HD], F32, name="gain")
+        fr = [keep.tile([P, HALF_T, 4 * PAIRS], BF16, name="fr%d" % i) for i in range(2)]
+        tab = [keep.tile([P, 2, HALF_T, HD], F32, name="tab%d" % i) for i in range(2)]
+        one = keep.tile([P, 1], F32, name="one")
+        one_out = keep.tile([P, 1], F32, name="one_out")
+
+        nc.vector.memset(bg[:], 0.0)
+        nc.vector.memset(xs[0][:].bitcast(I32), 0)
+        nc.vector.memset(ws[0][:].bitcast(I32), 0)
+        nc.vector.memset(one[:], 1.0)
+        nc.scalar.activation(out=one_out[:], in_=one[:], func=ACT.Abs_reciprocal_sqrt)
+        nc.gpsimd.dma_start(out=bg[0:HEADS, :], in_=b.rearrange("(h d) -> h d", d=HD))
+        nc.gpsimd.dma_start(out=bg[HEADS : HEADS + 1, :], in_=g.unsqueeze(0))
+        make_identity(nc, ident[:])
+        for i in range(2):
+            nc.gpsimd.dma_start(out=fr[i][:], in_=freqs_v[:, HALF_T * i : HALF_T * (i + 1), :])
+        nc.vector.memset(xs[1][:].bitcast(I32), 0)
+        nc.vector.memset(ws[1][:].bitcast(I32), 0)
+        for i in range(2, len(W_RANGES)):
+            nc.gpsimd.memset(ws[i][:].bitcast(I32), 0)
+
+        def load_x(i, g0, g1):
+            cols = slice(2 * HALF_TOK * i, 2 * HALF_TOK * (i + 1))
+            nc.sync.dma_start(
+                out=xc[i][:, g0:g1, :].bitcast(I32),
+                in_=x_words[g0:g1, :, cols].rearrange("g p c -> p g c").bitcast(I32),
+            )
+
+        def load_w(i, g0, g1):
+            c0, n = W_RANGES[i]
+            nc.sync.dma_start(
+                out=wc[i][:, g0:g1, :].bitcast(I32),
+                in_=w_words[g0:g1, :, 2 * c0 : 2 * (c0 + n)].rearrange("g p c -> p g c").bitcast(I32),
+            )
+
+        def load_scales(plane, src, c0, n):
+            for q in range(4):
+                nc.sync.dma_start(
+                    out=plane[32 * q : 32 * q + 4, :, :].bitcast(I32),
+                    in_=src[:, 4 * q : 4 * q + 4, c0 : c0 + n].rearrange("g r c -> r g c").bitcast(I32),
+                )
+
+        load_x(0, 0, 2)
+        load_w(0, 0, 2)
+        load_scales(xs[0], x_scales, 0, HALF_TOK)
+        load_scales(ws[0], w_scales, 0, 512)
+        load_x(0, 2, 5)
+        load_w(0, 2, 5)
+        load_x(0, 5, 8)
+        load_w(0, 5, 8)
+        load_x(1, 0, 8)
+        load_scales(xs[1], x_scales, HALF_TOK, HALF_TOK)
+        for i in range(1, len(W_RANGES)):
+            load_w(i, 0, 8)
+            load_scales(ws[i], w_scales, W_RANGES[i][0], W_RANGES[i][1])
+
+        gacc = psum.tile([P, BLOCK], F32, name="acc")
+        nc.tensor.matmul(gacc[:, 0:HD], lhsT=ident[:, HEADS : HEADS + 1].to_broadcast([P, P]), rhs=bg[:], start=True, stop=True)
+        nc.scalar.copy(gain[:], gacc[:, 0:HD])
+        for blk in range(C // BLOCK):
+            bacc = psum.tile([P, BLOCK], F32, name="acc")
+            for h in range(HEADS_BLOCK):
+                k = HEADS_BLOCK * blk + h
+                nc.tensor.matmul(
+                    bacc[:, HD * h : HD * (h + 1)],
+                    lhsT=ident[:, k : k + 1].to_broadcast([P, P]),
+                    rhs=bg[:],
+                    start=True,
+                    stop=True,
+                )
+            nc.scalar.copy(bias[:, blk, :], bacc[:])
+
+        def build_table(i):
+            for c in range(2):
+                nc.vector.tensor_tensor(
+                    out=tab[i][:, c, :, :].rearrange("p t (j i) -> p t j i", i=2),
+                    in0=fr[i][:].rearrange("p t (j i c) -> p t j i c", i=2, c=2)[:, :, :, :, c],
+                    in1=gain[:].rearrange("p (j c) -> p j c", c=2)[:, :, c].unsqueeze(1).unsqueeze(3).to_broadcast([P, HALF_T, PAIRS, 2]),
+                    op=MULT,
+                )
+
+        build_table(0)
+        build_table(1)
+
+        def mx_pass(acc, t, blk, k):
+            i, tt = divmod(t, HALF_T)
+            r = max(j for j in range(len(W_RANGES)) if W_RANGES[j][0] <= BLOCK * blk)
+            c0 = BLOCK * blk - W_RANGES[r][0]
+            nc.tensor.matmul_mx(
+                out=acc[:],
+                lhsT=xc[i][:, k, 2 * P * tt : 2 * P * (tt + 1)].bitcast(FP4X4),
+                lhsT_scale=xs[i][:, k, P * tt : P * (tt + 1)],
+                rhs=wc[r][:, k, 2 * c0 : 2 * (c0 + BLOCK)].bitcast(FP4X4),
+                rhs_scale=ws[r][:, k, c0 : c0 + BLOCK],
+                start=(k == 0),
+                stop=(k == GROUPS - 1),
+            )
+
+        for q, (blk, t0, n) in enumerate(CHUNKS):
+            accs = []
+            for i in range(n):
+                acc = psum.tile([P, BLOCK], F32, name="acc")
+                accs.append(acc)
+            if q == 0:
+                for k in range(GROUPS):
+                    for i in range(n):
+                        mx_pass(accs[i], t0 + i, blk, k)
+            else:
+                for i in range(n):
+                    for k in range(GROUPS):
+                        mx_pass(accs[i], t0 + i, blk, k)
+
+            u = work.tile([P, 4, BLOCK], F32, name="u")
+            s0 = work.tile([P, 4, BLOCK], F32, name="s0", bufs=3)
+            s1 = work.tile([P, 4, BLOCK], F32, name="s1")
+            ss = small.tile([P, 16], F32, name="ss")
+            rs = small.tile([P, 16], F32, name="rs")
+            for i in range(n):
+                nc.vector.tensor_tensor(out=u[:, i, :], in0=accs[i][:], in1=bias[:, blk, :], op=ADD)
+            for i in range(n):
+                for h in range(HEADS_BLOCK):
+                    k = HEADS_BLOCK * i + h
+                    junk = small.tile([P, HD], F32, name="junk")
+                    nc.scalar.activation(
+                        out=junk[:], in_=u[:, i, HD * h : HD * (h + 1)], func=ACT.Square, accum_out=ss[:, k : k + 1]
+                    )
+            nh = HEADS_BLOCK * n
+            nc.scalar.activation(out=rs[:, 0:nh], in_=ss[:, 0:nh], func=ACT.Abs_reciprocal_sqrt, scale=1.0 / HD, bias=EPS)
+
+            if n == 1:
+                halves = [(0, 1, 0, 2), (0, 1, 2, 2)]
+            else:
+                halves = [(0, n // 2, 0, HEADS_BLOCK), (n // 2, n // 2, 0, HEADS_BLOCK)]
+
+            def part(tile, half):
+                i0, m, h0, hn = half
+                return tile[:, i0 : i0 + m, HD * h0 : HD * (h0 + hn)]
+
+            def product(dst, c, half):
+                i0, m, h0, hn = half
+                i, tt = divmod(t0 + i0, HALF_T)
+                shape = [P, m, hn, PAIRS, 2]
+                nc.vector.tensor_tensor(
+                    out=part(dst, half).rearrange("p m (h j i) -> p m h j i", j=PAIRS, i=2),
+                    in0=part(u, half).rearrange("p m (h j c) -> p m h j c", j=PAIRS, c=2)[:, :, :, :, c : c + 1].to_broadcast(shape),
+                    in1=tab[i][:, c, tt : tt + m, :].rearrange("p m (j i) -> p m j i", i=2).unsqueeze(2).to_broadcast(shape),
+                    op=MULT,
+                )
+
+            def add(engine, half):
+                engine.tensor_tensor(out=part(s0, half), in0=part(s0, half), in1=part(s1, half), op=ADD)
+
+            ha, hb = halves
+            if n == 1:
+                product(s0, 0, ha)
+                product(s0, 0, hb)
+                product(s1, 1, ha)
+                product(s1, 1, hb)
+                add(nc.vector, ha)
+                add(nc.vector, hb)
+            else:
+                product(s0, 0, ha)
+                product(s1, 1, ha)
+                product(s0, 0, hb)
+                add(nc.vector, ha)
+                product(s1, 1, hb)
+                add(nc.gpsimd, hb)
+
+            for half in halves:
+                i0, m, h0, hn = half
+                for i in range(i0, i0 + m):
+                    for h in range(h0, h0 + hn):
+                        k = HEADS_BLOCK * i + h
+                        nc.scalar.activation(
+                            out=s0[:, i, HD * h : HD * (h + 1)],
+                            in_=s0[:, i, HD * h : HD * (h + 1)],
+                            func=ACT.Copy,
+                            scale=rs[:, k : k + 1],
+                        )
+                nc.sync.dma_start(
+                    out=out_v[:, t0 + i0 : t0 + i0 + m, BLOCK * blk + HD * h0 : BLOCK * blk + HD * (h0 + hn)],
+                    in_=part(s0, half),
+                )

@@ -30,11 +30,7 @@ FLOPS = 2 * TOKENS * C * C
 
 W_RANGES = [(0, 512), (512, 512), (1024, 1024), (2048, 1024), (3072, 1024)]
 
-CHUNKS = (
-    [(0, 0, 2), (0, 2, 2), (0, 4, 4)]
-    + [(blk, t0, 4) for blk in range(1, 7) for t0 in (0, 4)]
-    + [(7, 0, 4), (7, 4, 2), (7, 6, 1), (7, 7, 1)]
-)
+UNITS = [(blk, t0, 2) for blk in range(8) for t0 in (0, 2, 4, 6)][:-1] + [(7, 6, 1), (7, 7, 1)]
 
 
 def tile_selfattention_pa_kernel(tc, x_words, x_scales, freqs, w_words, w_scales, b, g, out):
@@ -66,16 +62,17 @@ def tile_selfattention_pa_kernel(tc, x_words, x_scales, freqs, w_words, w_scales
         nc.vector.memset(xs[0][:].bitcast(I32), 0)
         nc.vector.memset(ws[0][:].bitcast(I32), 0)
         nc.vector.memset(one[:], 1.0)
+        nc.scalar.dma_start(out=bg[0:HEADS, :], in_=b.rearrange("(h d) -> h d", d=HD))
+        nc.scalar.dma_start(out=bg[HEADS : HEADS + 1, :], in_=g.unsqueeze(0))
         nc.scalar.activation(out=one_out[:], in_=one[:], func=ACT.Abs_reciprocal_sqrt)
-        nc.gpsimd.dma_start(out=bg[0:HEADS, :], in_=b.rearrange("(h d) -> h d", d=HD))
-        nc.gpsimd.dma_start(out=bg[HEADS : HEADS + 1, :], in_=g.unsqueeze(0))
         make_identity(nc, ident[:])
-        for i in range(2):
-            nc.gpsimd.dma_start(out=fr[i][:], in_=freqs_v[:, HALF_T * i : HALF_T * (i + 1), :])
+        nc.gpsimd.dma_start(out=fr[0][:], in_=freqs_v[:, 0:HALF_T, :])
         nc.vector.memset(xs[1][:].bitcast(I32), 0)
         nc.vector.memset(ws[1][:].bitcast(I32), 0)
-        for i in range(2, len(W_RANGES)):
-            nc.gpsimd.memset(ws[i][:].bitcast(I32), 0)
+        nc.gpsimd.memset(ws[2][:].bitcast(I32), 0)
+        nc.gpsimd.dma_start(out=fr[1][:], in_=freqs_v[:, HALF_T:TILES, :])
+        nc.gpsimd.memset(ws[3][:].bitcast(I32), 0)
+        nc.gpsimd.memset(ws[4][:].bitcast(I32), 0)
 
         def load_x(i, g0, g1):
             cols = slice(2 * HALF_TOK * i, 2 * HALF_TOK * (i + 1))
@@ -106,11 +103,13 @@ def tile_selfattention_pa_kernel(tc, x_words, x_scales, freqs, w_words, w_scales
         load_w(0, 2, 5)
         load_x(0, 5, 8)
         load_w(0, 5, 8)
-        load_x(1, 0, 8)
         load_scales(xs[1], x_scales, HALF_TOK, HALF_TOK)
+        load_x(1, 0, 4)
+        load_x(1, 4, 8)
         for i in range(1, len(W_RANGES)):
-            load_w(i, 0, 8)
             load_scales(ws[i], w_scales, W_RANGES[i][0], W_RANGES[i][1])
+            load_w(i, 0, 4)
+            load_w(i, 4, 8)
 
         gacc = psum.tile([P, BLOCK], F32, name="acc")
         nc.tensor.matmul(gacc[:, 0:HD], lhsT=ident[:, HEADS : HEADS + 1].to_broadcast([P, P]), rhs=bg[:], start=True, stop=True)
@@ -154,12 +153,16 @@ def tile_selfattention_pa_kernel(tc, x_words, x_scales, freqs, w_words, w_scales
                 stop=(k == GROUPS - 1),
             )
 
-        for q, (blk, t0, n) in enumerate(CHUNKS):
+        def part(tile, tiles):
+            return tile[:, tiles[0] : tiles[1], :]
+
+        def multiply(unit):
+            blk, t0, n = unit
             accs = []
             for i in range(n):
                 acc = psum.tile([P, BLOCK], F32, name="acc")
                 accs.append(acc)
-            if q == 0:
+            if blk == 0 and t0 == 0:
                 for k in range(GROUPS):
                     for i in range(n):
                         mx_pass(accs[i], t0 + i, blk, k)
@@ -167,12 +170,52 @@ def tile_selfattention_pa_kernel(tc, x_words, x_scales, freqs, w_words, w_scales
                 for i in range(n):
                     for k in range(GROUPS):
                         mx_pass(accs[i], t0 + i, blk, k)
+            return accs
 
-            u = work.tile([P, 4, BLOCK], F32, name="u")
-            s0 = work.tile([P, 4, BLOCK], F32, name="s0", bufs=3)
-            s1 = work.tile([P, 4, BLOCK], F32, name="s1")
-            ss = small.tile([P, 16], F32, name="ss")
-            rs = small.tile([P, 16], F32, name="rs")
+        def add(engine, st, tiles):
+            if tiles[1] > tiles[0]:
+                engine.tensor_tensor(out=part(st["s0"], tiles), in0=part(st["s0"], tiles), in1=part(st["s1"], tiles), op=ADD)
+
+        def product(dst, c, u, unit):
+            blk, t0, n = unit
+            i, tt = divmod(t0, HALF_T)
+            shape = [P, n, HEADS_BLOCK, PAIRS, 2]
+            nc.vector.tensor_tensor(
+                out=part(dst, (0, n)).rearrange("p m (h j i) -> p m h j i", j=PAIRS, i=2),
+                in0=part(u, (0, n)).rearrange("p m (h j c) -> p m h j c", j=PAIRS, c=2)[:, :, :, :, c : c + 1].to_broadcast(shape),
+                in1=tab[i][:, c, tt : tt + n, :].rearrange("p m (j i) -> p m j i", i=2).unsqueeze(2).to_broadcast(shape),
+                op=MULT,
+            )
+
+        def finish(st, tiles):
+            blk, t0, n = st["unit"]
+            for i in range(tiles[0], tiles[1]):
+                for h in range(HEADS_BLOCK):
+                    k = HEADS_BLOCK * i + h
+                    nc.scalar.activation(
+                        out=st["s0"][:, i, HD * h : HD * (h + 1)],
+                        in_=st["s0"][:, i, HD * h : HD * (h + 1)],
+                        func=ACT.Copy,
+                        scale=st["rs"][:, k : k + 1],
+                    )
+            if tiles[1] > tiles[0]:
+                nc.sync.dma_start(
+                    out=out_v[:, t0 + tiles[0] : t0 + tiles[1], BLOCK * blk : BLOCK * (blk + 1)],
+                    in_=part(st["s0"], tiles),
+                )
+
+        def shares(n):
+            return ((0, n), (n, n))
+
+        prev = None
+        for unit in UNITS:
+            blk, t0, n = unit
+            accs = multiply(unit)
+            u = work.tile([P, 2, BLOCK], F32, name="u", bufs=3)
+            s0 = work.tile([P, 2, BLOCK], F32, name="s0", bufs=5)
+            s1 = work.tile([P, 2, BLOCK], F32, name="s1", bufs=3)
+            ss = small.tile([P, 8], F32, name="ss")
+            rs = small.tile([P, 8], F32, name="rs")
             for i in range(n):
                 nc.vector.tensor_tensor(out=u[:, i, :], in0=accs[i][:], in1=bias[:, blk, :], op=ADD)
             for i in range(n):
@@ -184,58 +227,16 @@ def tile_selfattention_pa_kernel(tc, x_words, x_scales, freqs, w_words, w_scales
                     )
             nh = HEADS_BLOCK * n
             nc.scalar.activation(out=rs[:, 0:nh], in_=ss[:, 0:nh], func=ACT.Abs_reciprocal_sqrt, scale=1.0 / HD, bias=EPS)
-
-            if n == 1:
-                halves = [(0, 1, 0, 2), (0, 1, 2, 2)]
-            else:
-                halves = [(0, n // 2, 0, HEADS_BLOCK), (n // 2, n // 2, 0, HEADS_BLOCK)]
-
-            def part(tile, half):
-                i0, m, h0, hn = half
-                return tile[:, i0 : i0 + m, HD * h0 : HD * (h0 + hn)]
-
-            def product(dst, c, half):
-                i0, m, h0, hn = half
-                i, tt = divmod(t0 + i0, HALF_T)
-                shape = [P, m, hn, PAIRS, 2]
-                nc.vector.tensor_tensor(
-                    out=part(dst, half).rearrange("p m (h j i) -> p m h j i", j=PAIRS, i=2),
-                    in0=part(u, half).rearrange("p m (h j c) -> p m h j c", j=PAIRS, c=2)[:, :, :, :, c : c + 1].to_broadcast(shape),
-                    in1=tab[i][:, c, tt : tt + m, :].rearrange("p m (j i) -> p m j i", i=2).unsqueeze(2).to_broadcast(shape),
-                    op=MULT,
-                )
-
-            def add(engine, half):
-                engine.tensor_tensor(out=part(s0, half), in0=part(s0, half), in1=part(s1, half), op=ADD)
-
-            ha, hb = halves
-            if n == 1:
-                product(s0, 0, ha)
-                product(s0, 0, hb)
-                product(s1, 1, ha)
-                product(s1, 1, hb)
-                add(nc.vector, ha)
-                add(nc.vector, hb)
-            else:
-                product(s0, 0, ha)
-                product(s1, 1, ha)
-                product(s0, 0, hb)
-                add(nc.vector, ha)
-                product(s1, 1, hb)
-                add(nc.gpsimd, hb)
-
-            for half in halves:
-                i0, m, h0, hn = half
-                for i in range(i0, i0 + m):
-                    for h in range(h0, h0 + hn):
-                        k = HEADS_BLOCK * i + h
-                        nc.scalar.activation(
-                            out=s0[:, i, HD * h : HD * (h + 1)],
-                            in_=s0[:, i, HD * h : HD * (h + 1)],
-                            func=ACT.Copy,
-                            scale=rs[:, k : k + 1],
-                        )
-                nc.sync.dma_start(
-                    out=out_v[:, t0 + i0 : t0 + i0 + m, BLOCK * blk + HD * h0 : BLOCK * blk + HD * (h0 + hn)],
-                    in_=part(s0, half),
-                )
+            if prev is not None:
+                own, other = shares(prev["unit"][2])
+                add(nc.vector, prev, own)
+                finish(prev, other)
+                finish(prev, own)
+            product(s0, 0, u, unit)
+            product(s1, 1, u, unit)
+            prev = {"unit": unit, "s0": s0, "s1": s1, "rs": rs}
+            own, other = shares(n)
+            add(nc.gpsimd, prev, other)
+        own, other = shares(prev["unit"][2])
+        add(nc.vector, prev, own)
+        finish(prev, own)

@@ -42,7 +42,8 @@ def tile_selfattention_pa_kernel(tc, x_words, x_scales, freqs, w_words, w_scales
         keep = ctx.enter_context(tc.tile_pool(name="keep", bufs=1))
         work = ctx.enter_context(tc.tile_pool(name="work", bufs=2))
         small = ctx.enter_context(tc.tile_pool(name="small", bufs=3))
-        psum = ctx.enter_context(tc.psum_pool(name="psum", bufs=8))
+        psum = ctx.enter_context(tc.psum_pool(name="psum", bufs=4))
+        psum_tab = ctx.enter_context(tc.psum_pool(name="psum_tab", bufs=1))
         ctx.enter_context(tc.manual_schedule())
 
         xc = [keep.tile([P, GROUPS, 2 * HALF_TOK], U8, name="xc%d" % i, align_bytes=64) for i in range(2)]
@@ -55,6 +56,8 @@ def tile_selfattention_pa_kernel(tc, x_words, x_scales, freqs, w_words, w_scales
         gain = keep.tile([P, HD], F32, name="gain")
         fr = [keep.tile([P, HALF_T, 4 * PAIRS], BF16, name="fr%d" % i) for i in range(2)]
         tab = [keep.tile([P, 2, HALF_T, HD], F32, name="tab%d" % i) for i in range(2)]
+        hi = [keep.tile([P, 2, HALF_T, HD], BF16, name="hi%d" % i) for i in range(2)]
+        lo = [keep.tile([P, 2, HALF_T, HD], BF16, name="lo%d" % i) for i in range(2)]
         one = keep.tile([P, 1], F32, name="one")
         one_out = keep.tile([P, 1], F32, name="one_out")
 
@@ -115,7 +118,10 @@ def tile_selfattention_pa_kernel(tc, x_words, x_scales, freqs, w_words, w_scales
         nc.tensor.matmul(gacc[:, 0:HD], lhsT=ident[:, HEADS : HEADS + 1].to_broadcast([P, P]), rhs=bg[:], start=True, stop=True)
         nc.scalar.copy(gain[:], gacc[:, 0:HD])
         for blk in range(C // BLOCK):
-            bacc = psum.tile([P, BLOCK], F32, name="acc")
+            if 3 <= blk < 7:
+                bacc = psum_tab.tile([P, BLOCK], F32, name="ptab%d" % (blk - 3))
+            else:
+                bacc = psum.tile([P, BLOCK], F32, name="acc")
             for h in range(HEADS_BLOCK):
                 k = HEADS_BLOCK * blk + h
                 nc.tensor.matmul(
@@ -136,8 +142,22 @@ def tile_selfattention_pa_kernel(tc, x_words, x_scales, freqs, w_words, w_scales
                     op=MULT,
                 )
 
-        build_table(0)
-        build_table(1)
+        def split_table(i):
+            nc.vector.tensor_copy(out=hi[i][:], in_=tab[i][:])
+            nc.vector.tensor_tensor(out=lo[i][:], in0=tab[i][:], in1=hi[i][:], op=mybir.AluOpType.subtract)
+
+        ptab = [[None, None], [None, None]]
+
+        def place_table(i):
+            for c in range(2):
+                bank = psum_tab.tile([P, BLOCK], F32, name="ptab%d" % (2 * i + c))
+                nc.tensor.matmul(bank[:], lhsT=ident[:], rhs=hi[i][:, c, :, :].rearrange("p t d -> p (t d)"), start=True, stop=False)
+                nc.tensor.matmul(bank[:], lhsT=ident[:], rhs=lo[i][:, c, :, :].rearrange("p t d -> p (t d)"), start=False, stop=True)
+                ptab[i][c] = bank
+
+        for i in range(2):
+            build_table(i)
+            split_table(i)
 
         def mx_pass(acc, t, blk, k):
             i, tt = divmod(t, HALF_T)
@@ -176,14 +196,18 @@ def tile_selfattention_pa_kernel(tc, x_words, x_scales, freqs, w_words, w_scales
             if tiles[1] > tiles[0]:
                 engine.tensor_tensor(out=part(st["s0"], tiles), in0=part(st["s0"], tiles), in1=part(st["s1"], tiles), op=ADD)
 
-        def product(dst, c, u, unit):
+        def product(dst, c, u, unit, tiles):
             blk, t0, n = unit
-            i, tt = divmod(t0, HALF_T)
-            shape = [P, n, HEADS_BLOCK, PAIRS, 2]
+            i, tt = divmod(t0 + tiles[0], HALF_T)
+            m = tiles[1] - tiles[0]
+            shape = [P, m, HEADS_BLOCK, PAIRS, 2]
             nc.vector.tensor_tensor(
-                out=part(dst, (0, n)).rearrange("p m (h j i) -> p m h j i", j=PAIRS, i=2),
-                in0=part(u, (0, n)).rearrange("p m (h j c) -> p m h j c", j=PAIRS, c=2)[:, :, :, :, c : c + 1].to_broadcast(shape),
-                in1=tab[i][:, c, tt : tt + n, :].rearrange("p m (j i) -> p m j i", i=2).unsqueeze(2).to_broadcast(shape),
+                out=part(dst, tiles).rearrange("p m (h j i) -> p m h j i", j=PAIRS, i=2),
+                in0=part(u, tiles).rearrange("p m (h j c) -> p m h j c", j=PAIRS, c=2)[:, :, :, :, c : c + 1].to_broadcast(shape),
+                in1=ptab[i][c][:, HD * tt : HD * (tt + m)]
+                .rearrange("p (m j i) -> p m j i", j=PAIRS, i=2)
+                .unsqueeze(2)
+                .to_broadcast(shape),
                 op=MULT,
             )
 
@@ -204,39 +228,34 @@ def tile_selfattention_pa_kernel(tc, x_words, x_scales, freqs, w_words, w_scales
                     in_=part(st["s0"], tiles),
                 )
 
-        def shares(n):
-            return ((0, n), (n, n))
-
         prev = None
-        for unit in UNITS:
+        for q, unit in enumerate(UNITS):
             blk, t0, n = unit
             accs = multiply(unit)
+            if q < 2:
+                place_table(q)
             u = work.tile([P, 2, BLOCK], F32, name="u", bufs=3)
             s0 = work.tile([P, 2, BLOCK], F32, name="s0", bufs=5)
             s1 = work.tile([P, 2, BLOCK], F32, name="s1", bufs=3)
             ss = small.tile([P, 8], F32, name="ss")
             rs = small.tile([P, 8], F32, name="rs")
             for i in range(n):
-                nc.vector.tensor_tensor(out=u[:, i, :], in0=accs[i][:], in1=bias[:, blk, :], op=ADD)
+                nc.vector.tensor_tensor(out=u[:, i, :], in0=bias[:, blk, :], in1=accs[i][:], op=ADD)
             for i in range(n):
                 for h in range(HEADS_BLOCK):
                     k = HEADS_BLOCK * i + h
-                    junk = small.tile([P, HD], F32, name="junk")
+                    junk = small.tile([P, HD], F32, name="junk", bufs=4)
                     nc.scalar.activation(
                         out=junk[:], in_=u[:, i, HD * h : HD * (h + 1)], func=ACT.Square, accum_out=ss[:, k : k + 1]
                     )
             nh = HEADS_BLOCK * n
             nc.scalar.activation(out=rs[:, 0:nh], in_=ss[:, 0:nh], func=ACT.Abs_reciprocal_sqrt, scale=1.0 / HD, bias=EPS)
             if prev is not None:
-                own, other = shares(prev["unit"][2])
-                add(nc.vector, prev, own)
-                finish(prev, other)
-                finish(prev, own)
-            product(s0, 0, u, unit)
-            product(s1, 1, u, unit)
+                finish(prev, (0, prev["unit"][2]))
+            for i in range(n):
+                product(s0, 0, u, unit, (i, i + 1))
+            product(s1, 1, u, unit, (0, n))
             prev = {"unit": unit, "s0": s0, "s1": s1, "rs": rs}
-            own, other = shares(n)
-            add(nc.gpsimd, prev, other)
-        own, other = shares(prev["unit"][2])
-        add(nc.vector, prev, own)
-        finish(prev, own)
+            last = q == len(UNITS) - 1
+            add(nc.vector if last else nc.gpsimd, prev, (0, n))
+        finish(prev, (0, prev["unit"][2]))

@@ -28,6 +28,10 @@ HALF_TOK = HALF_T * P
 
 FLOPS = 2 * TOKENS * C * C
 
+WARM_MATMULS = 14
+
+HEAD_BLOCKS = 4
+
 W_RANGES = [(0, 512), (512, 512), (1024, 1024), (2048, 1024), (3072, 1024)]
 
 UNITS = [(blk, t0, 2) for blk in range(8) for t0 in (0, 2, 4, 6)][:-1] + [(7, 6, 1), (7, 7, 1)]
@@ -52,7 +56,8 @@ def tile_selfattention_pa_kernel(tc, x_words, x_scales, freqs, w_words, w_scales
         ws = [keep.tile([P, GROUPS, n], U8, name="ws%d" % i, align_bytes=64) for i, (c0, n) in enumerate(W_RANGES)]
         bg = keep.tile([P, HD], BF16, name="bg")
         ident = keep.tile([P, P], BF16, name="ident")
-        bias = keep.tile([P, C // BLOCK, BLOCK], F32, name="bias")
+        bias = keep.tile([P, HEAD_BLOCKS, BLOCK], F32, name="bias")
+        bias_late = keep.tile([P, C // BLOCK - HEAD_BLOCKS, BLOCK], BF16, name="bias_late")
         gain = keep.tile([P, HD], F32, name="gain")
         fr = [keep.tile([P, HALF_T, 4 * PAIRS], BF16, name="fr%d" % i) for i in range(2)]
         tab = [keep.tile([P, 2, HALF_T, HD], F32, name="tab%d" % i) for i in range(2)]
@@ -69,10 +74,10 @@ def tile_selfattention_pa_kernel(tc, x_words, x_scales, freqs, w_words, w_scales
         nc.scalar.dma_start(out=bg[HEADS : HEADS + 1, :], in_=g.unsqueeze(0))
         nc.scalar.activation(out=one_out[:], in_=one[:], func=ACT.Abs_reciprocal_sqrt)
         make_identity(nc, ident[:])
-        nc.gpsimd.dma_start(out=fr[0][:], in_=freqs_v[:, 0:HALF_T, :])
         nc.vector.memset(xs[1][:].bitcast(I32), 0)
         nc.vector.memset(ws[1][:].bitcast(I32), 0)
         nc.gpsimd.memset(ws[2][:].bitcast(I32), 0)
+        nc.gpsimd.dma_start(out=fr[0][:], in_=freqs_v[:, 0:HALF_T, :])
         nc.gpsimd.dma_start(out=fr[1][:], in_=freqs_v[:, HALF_T:TILES, :])
         nc.gpsimd.memset(ws[3][:].bitcast(I32), 0)
         nc.gpsimd.memset(ws[4][:].bitcast(I32), 0)
@@ -91,37 +96,41 @@ def tile_selfattention_pa_kernel(tc, x_words, x_scales, freqs, w_words, w_scales
                 in_=w_words[g0:g1, :, 2 * c0 : 2 * (c0 + n)].rearrange("g p c -> p g c").bitcast(I32),
             )
 
-        def load_scales(plane, src, c0, n):
+        def load_scales(plane, src, c0, n, g0, g1):
             for q in range(4):
                 nc.sync.dma_start(
-                    out=plane[32 * q : 32 * q + 4, :, :].bitcast(I32),
-                    in_=src[:, 4 * q : 4 * q + 4, c0 : c0 + n].rearrange("g r c -> r g c").bitcast(I32),
+                    out=plane[32 * q : 32 * q + 4, g0:g1, :].bitcast(I32),
+                    in_=src[g0:g1, 4 * q : 4 * q + 4, c0 : c0 + n].rearrange("g r c -> r g c").bitcast(I32),
                 )
 
-        load_x(0, 0, 2)
-        load_w(0, 0, 2)
-        load_scales(xs[0], x_scales, 0, HALF_TOK)
-        load_scales(ws[0], w_scales, 0, 512)
-        load_x(0, 2, 5)
-        load_w(0, 2, 5)
-        load_x(0, 5, 8)
-        load_w(0, 5, 8)
-        load_scales(xs[1], x_scales, HALF_TOK, HALF_TOK)
-        load_x(1, 0, 4)
-        load_x(1, 4, 8)
-        for i in range(1, len(W_RANGES)):
-            load_scales(ws[i], w_scales, W_RANGES[i][0], W_RANGES[i][1])
+        def load_range(i):
+            load_scales(ws[i], w_scales, W_RANGES[i][0], W_RANGES[i][1], 0, 8)
             load_w(i, 0, 4)
             load_w(i, 4, 8)
 
+        load_x(0, 0, 2)
+        load_w(0, 0, 2)
+        load_scales(xs[0], x_scales, 0, HALF_TOK, 0, 4)
+        load_scales(ws[0], w_scales, 0, 512, 0, 4)
+        load_x(0, 2, 4)
+        load_w(0, 2, 4)
+        load_scales(xs[0], x_scales, 0, HALF_TOK, 4, 8)
+        load_scales(ws[0], w_scales, 0, 512, 4, 8)
+        load_x(0, 4, 8)
+        load_w(0, 4, 8)
+        load_scales(xs[1], x_scales, HALF_TOK, HALF_TOK, 0, 8)
+        load_x(1, 0, 4)
+        load_x(1, 4, 8)
+        load_range(1)
+
+        warm = psum_tab.tile([P, BLOCK], F32, name="ptab0")
+        for i in range(WARM_MATMULS):
+            nc.tensor.matmul(warm[:, 0:P], lhsT=ident[:], rhs=ident[:], start=True, stop=True)
         gacc = psum.tile([P, BLOCK], F32, name="acc")
         nc.tensor.matmul(gacc[:, 0:HD], lhsT=ident[:, HEADS : HEADS + 1].to_broadcast([P, P]), rhs=bg[:], start=True, stop=True)
         nc.scalar.copy(gain[:], gacc[:, 0:HD])
-        for blk in range(C // BLOCK):
-            if 3 <= blk < 7:
-                bacc = psum_tab.tile([P, BLOCK], F32, name="ptab%d" % (blk - 3))
-            else:
-                bacc = psum.tile([P, BLOCK], F32, name="acc")
+        def spread_bias(blk):
+            bacc = psum.tile([P, BLOCK], F32, name="acc")
             for h in range(HEADS_BLOCK):
                 k = HEADS_BLOCK * blk + h
                 nc.tensor.matmul(
@@ -133,12 +142,18 @@ def tile_selfattention_pa_kernel(tc, x_words, x_scales, freqs, w_words, w_scales
                 )
             nc.scalar.copy(bias[:, blk, :], bacc[:])
 
+        for blk in range(HEAD_BLOCKS):
+            spread_bias(blk)
+
         def build_table(i):
-            for c in range(2):
+            pairs = fr[i][:].rearrange("p t (j k) -> p t j k", k=4)
+            gains = gain[:].rearrange("p (j i) -> p j i", i=2)
+            shape = [P, HALF_T, PAIRS, 2]
+            for c, entries, gg in ((0, pairs[:, :, :, 0:4:3], gains), (1, pairs[:, :, :, 1:3], gains[:, :, ::-1])):
                 nc.vector.tensor_tensor(
                     out=tab[i][:, c, :, :].rearrange("p t (j i) -> p t j i", i=2),
-                    in0=fr[i][:].rearrange("p t (j i c) -> p t j i c", i=2, c=2)[:, :, :, :, c],
-                    in1=gain[:].rearrange("p (j c) -> p j c", c=2)[:, :, c].unsqueeze(1).unsqueeze(3).to_broadcast([P, HALF_T, PAIRS, 2]),
+                    in0=entries,
+                    in1=gg.unsqueeze(1).to_broadcast(shape),
                     op=MULT,
                 )
 
@@ -176,20 +191,30 @@ def tile_selfattention_pa_kernel(tc, x_words, x_scales, freqs, w_words, w_scales
         def part(tile, tiles):
             return tile[:, tiles[0] : tiles[1], :]
 
-        def multiply(unit):
-            blk, t0, n = unit
+        def new_accs(n):
             accs = []
             for i in range(n):
                 acc = psum.tile([P, BLOCK], F32, name="acc")
                 accs.append(acc)
-            if blk == 0 and t0 == 0:
+            return accs
+
+        def multiply(unit):
+            blk, t0, n = unit
+            accs = new_accs(n)
+            for i in range(n):
                 for k in range(GROUPS):
-                    for i in range(n):
-                        mx_pass(accs[i], t0 + i, blk, k)
-            else:
-                for i in range(n):
-                    for k in range(GROUPS):
-                        mx_pass(accs[i], t0 + i, blk, k)
+                    mx_pass(accs[i], t0 + i, blk, k)
+            return accs
+
+        def multiply_first():
+            accs = new_accs(4)
+            for k in range(GROUPS // 2):
+                for t in range(4):
+                    mx_pass(accs[t], t, 0, k)
+            place_table(0)
+            for t in range(4):
+                for k in range(GROUPS // 2, GROUPS):
+                    mx_pass(accs[t], t, 0, k)
             return accs
 
         def add(engine, st, tiles):
@@ -201,9 +226,10 @@ def tile_selfattention_pa_kernel(tc, x_words, x_scales, freqs, w_words, w_scales
             i, tt = divmod(t0 + tiles[0], HALF_T)
             m = tiles[1] - tiles[0]
             shape = [P, m, HEADS_BLOCK, PAIRS, 2]
+            channels = part(u, tiles).rearrange("p m (h j i) -> p m h j i", j=PAIRS, i=2)
             nc.vector.tensor_tensor(
                 out=part(dst, tiles).rearrange("p m (h j i) -> p m h j i", j=PAIRS, i=2),
-                in0=part(u, tiles).rearrange("p m (h j c) -> p m h j c", j=PAIRS, c=2)[:, :, :, :, c : c + 1].to_broadcast(shape),
+                in0=channels if c == 0 else channels[:, :, :, :, ::-1],
                 in1=ptab[i][c][:, HD * tt : HD * (tt + m)]
                 .rearrange("p (m j i) -> p m j i", j=PAIRS, i=2)
                 .unsqueeze(2)
@@ -231,16 +257,18 @@ def tile_selfattention_pa_kernel(tc, x_words, x_scales, freqs, w_words, w_scales
         prev = None
         for q, unit in enumerate(UNITS):
             blk, t0, n = unit
-            accs = multiply(unit)
-            if q < 2:
-                place_table(q)
+            if q == 0:
+                first = multiply_first()
+                place_table(1)
+            accs = first[2 * q : 2 * q + 2] if q < 2 else multiply(unit)
             u = work.tile([P, 2, BLOCK], F32, name="u", bufs=3)
             s0 = work.tile([P, 2, BLOCK], F32, name="s0", bufs=5)
             s1 = work.tile([P, 2, BLOCK], F32, name="s1", bufs=3)
             ss = small.tile([P, 8], F32, name="ss")
             rs = small.tile([P, 8], F32, name="rs")
+            row = bias[:, blk, :] if blk < HEAD_BLOCKS else bias_late[:, blk - HEAD_BLOCKS, :]
             for i in range(n):
-                nc.vector.tensor_tensor(out=u[:, i, :], in0=bias[:, blk, :], in1=accs[i][:], op=ADD)
+                nc.vector.tensor_tensor(out=u[:, i, :], in0=row, in1=accs[i][:], op=ADD)
             for i in range(n):
                 for h in range(HEADS_BLOCK):
                     k = HEADS_BLOCK * i + h
@@ -250,12 +278,27 @@ def tile_selfattention_pa_kernel(tc, x_words, x_scales, freqs, w_words, w_scales
                     )
             nh = HEADS_BLOCK * n
             nc.scalar.activation(out=rs[:, 0:nh], in_=ss[:, 0:nh], func=ACT.Abs_reciprocal_sqrt, scale=1.0 / HD, bias=EPS)
+            if q == 1:
+                load_range(2)
+            if q == 5:
+                nc.sync.dma_start(
+                    out=bias_late[:].rearrange("p c n -> p (c n)"), in_=b[BLOCK * HEAD_BLOCKS : C].partition_broadcast(P)
+                )
+            if q in (8, 16):
+                load_range(3 if q == 8 else 4)
             if prev is not None:
                 finish(prev, (0, prev["unit"][2]))
             for i in range(n):
                 product(s0, 0, u, unit, (i, i + 1))
             product(s1, 1, u, unit, (0, n))
             prev = {"unit": unit, "s0": s0, "s1": s1, "rs": rs}
-            last = q == len(UNITS) - 1
-            add(nc.vector if last else nc.gpsimd, prev, (0, n))
-        finish(prev, (0, prev["unit"][2]))
+            if q < len(UNITS) - 1:
+                add(nc.gpsimd, prev, (0, n))
+        blk, t0, n = prev["unit"]
+        for c0 in (0, 2 * HD):
+            cols = slice(c0, c0 + 2 * HD)
+            nc.vector.tensor_tensor(out=s0[:, 0, cols], in0=s0[:, 0, cols], in1=s1[:, 0, cols], op=ADD)
+            for h in range(c0 // HD, c0 // HD + 2):
+                hc = slice(HD * h, HD * (h + 1))
+                nc.scalar.activation(out=s0[:, 0, hc], in_=s0[:, 0, hc], func=ACT.Copy, scale=rs[:, h : h + 1])
+            nc.sync.dma_start(out=out_v[:, t0, BLOCK * blk + c0 : BLOCK * blk + c0 + 2 * HD], in_=s0[:, 0, cols])

from contextlib import ExitStack

import concourse.mybir as mybir
from concourse.masks import make_identity

F32 = mybir.dt.float32
BF16 = mybir.dt.bfloat16
I32 = mybir.dt.int32
U8 = mybir.dt.uint8
FP4X4 = mybir.dt.float4_e2m1fn_x4
ADD = mybir.AluOpType.add
MULT = mybir.AluOpType.mult
ACT = mybir.ActivationFunctionType

P = 128
TOKENS = 1024
C = 4096
GROUPS = C // 512
HD = 128
HEADS = C // HD
PAIRS = HD // 2
EPS = 1e-6
BLOCK = 512
HEADS_BLOCK = BLOCK // HD
TILES = TOKENS // P
HALF_T = TILES // 2
HALF_TOK = HALF_T * P

FLOPS = 2 * TOKENS * C * C

WARM_MATMULS = 14

HEAD_BLOCKS = 4

W_RANGES = [(0, 512), (512, 512), (1024, 1024), (2048, 1024), (3072, 1024)]

UNITS = [(blk, t0, 2) for blk in range(8) for t0 in (0, 2, 4, 6)][:-1] + [(7, 6, 1), (7, 7, 1)]


def tile_selfattention_pa_kernel(tc, x_words, x_scales, freqs, w_words, w_scales, b, g, out):
    nc = tc.nc
    out_v = out.rearrange("a (t p) h d -> p (a t) (h d)", p=P)
    freqs_v = freqs.rearrange("a (t p) c j i k -> p (a t) (c j i k)", p=P)

    with ExitStack() as ctx:
        keep = ctx.enter_context(tc.tile_pool(name="keep", bufs=1))
        work = ctx.enter_context(tc.tile_pool(name="work", bufs=2))
        small = ctx.enter_context(tc.tile_pool(name="small", bufs=3))
        psum = ctx.enter_context(tc.psum_pool(name="psum", bufs=4))
        psum_tab = ctx.enter_context(tc.psum_pool(name="psum_tab", bufs=1))
        ctx.enter_context(tc.manual_schedule())

        xc = [keep.tile([P, GROUPS, 2 * HALF_TOK], U8, name="xc%d" % i, align_bytes=64) for i in range(2)]
        xs = [keep.tile([P, GROUPS, HALF_TOK], U8, name="xs%d" % i, align_bytes=64) for i in range(2)]
        wc = [keep.tile([P, GROUPS, 2 * n], U8, name="wc%d" % i, align_bytes=64) for i, (c0, n) in enumerate(W_RANGES)]
        ws = [keep.tile([P, GROUPS, n], U8, name="ws%d" % i, align_bytes=64) for i, (c0, n) in enumerate(W_RANGES)]
        bg = keep.tile([P, HD], BF16, name="bg")
        ident = keep.tile([P, P], BF16, name="ident")
        bias = keep.tile([P, HEAD_BLOCKS, BLOCK], F32, name="bias")
        bias_late = keep.tile([P, C // BLOCK - HEAD_BLOCKS, BLOCK], BF16, name="bias_late")
        gain = keep.tile([P, HD], F32, name="gain")
        fr = [keep.tile([P, HALF_T, 4 * PAIRS], BF16, name="fr%d" % i) for i in range(2)]
        tab = [keep.tile([P, 2, HALF_T, HD], F32, name="tab%d" % i) for i in range(2)]
        hi = [keep.tile([P, 2, HALF_T, HD], BF16, name="hi%d" % i) for i in range(2)]
        lo = [keep.tile([P, 2, HALF_T, HD], BF16, name="lo%d" % i) for i in range(2)]
        one = keep.tile([P, 1], F32, name="one")
        one_out = keep.tile([P, 1], F32, name="one_out")

        nc.vector.memset(bg[:], 0.0)
        nc.vector.memset(xs[0][:].bitcast(I32), 0)
        nc.vector.memset(ws[0][:].bitcast(I32), 0)
        nc.vector.memset(one[:], 1.0)
        nc.scalar.dma_start(out=bg[0:HEADS, :], in_=b.rearrange("(h d) -> h d", d=HD))
        nc.scalar.dma_start(out=bg[HEADS : HEADS + 1, :], in_=g.unsqueeze(0))
        nc.scalar.activation(out=one_out[:], in_=one[:], func=ACT.Abs_reciprocal_sqrt)
        make_identity(nc, ident[:])
        nc.vector.memset(xs[1][:].bitcast(I32), 0)
        nc.vector.memset(ws[1][:].bitcast(I32), 0)
        nc.gpsimd.memset(ws[2][:].bitcast(I32), 0)
        nc.gpsimd.dma_start(out=fr[0][:], in_=freqs_v[:, 0:HALF_T, :])
        nc.gpsimd.dma_start(out=fr[1][:], in_=freqs_v[:, HALF_T:TILES, :])
        nc.gpsimd.memset(ws[3][:].bitcast(I32), 0)
        nc.gpsimd.memset(ws[4][:].bitcast(I32), 0)

        def load_x(i, g0, g1):
            cols = slice(2 * HALF_TOK * i, 2 * HALF_TOK * (i + 1))
            nc.sync.dma_start(
                out=xc[i][:, g0:g1, :].bitcast(I32),
                in_=x_words[g0:g1, :, cols].rearrange("g p c -> p g c").bitcast(I32),
            )

        def load_w(i, g0, g1):
            c0, n = W_RANGES[i]
            nc.sync.dma_start(
                out=wc[i][:, g0:g1, :].bitcast(I32),
                in_=w_words[g0:g1, :, 2 * c0 : 2 * (c0 + n)].rearrange("g p c -> p g c").bitcast(I32),
            )

        def load_scales(plane, src, c0, n, g0, g1):
            for q in range(4):
                nc.sync.dma_start(
                    out=plane[32 * q : 32 * q + 4, g0:g1, :].bitcast(I32),
                    in_=src[g0:g1, 4 * q : 4 * q + 4, c0 : c0 + n].rearrange("g r c -> r g c").bitcast(I32),
                )

        def load_range(i):
            load_scales(ws[i], w_scales, W_RANGES[i][0], W_RANGES[i][1], 0, 8)
            load_w(i, 0, 4)
            load_w(i, 4, 8)

        load_x(0, 0, 2)
        load_w(0, 0, 2)
        load_scales(xs[0], x_scales, 0, HALF_TOK, 0, 4)
        load_scales(ws[0], w_scales, 0, 512, 0, 4)
        load_x(0, 2, 4)
        load_w(0, 2, 4)
        load_scales(xs[0], x_scales, 0, HALF_TOK, 4, 8)
        load_scales(ws[0], w_scales, 0, 512, 4, 8)
        load_x(0, 4, 8)
        load_w(0, 4, 8)
        load_scales(xs[1], x_scales, HALF_TOK, HALF_TOK, 0, 8)
        load_x(1, 0, 4)
        load_x(1, 4, 8)
        load_range(1)

        warm = psum_tab.tile([P, BLOCK], F32, name="ptab0")
        for i in range(WARM_MATMULS):
            nc.tensor.matmul(warm[:, 0:P], lhsT=ident[:], rhs=ident[:], start=True, stop=True)
        gacc = psum.tile([P, BLOCK], F32, name="acc")
        nc.tensor.matmul(gacc[:, 0:HD], lhsT=ident[:, HEADS : HEADS + 1].to_broadcast([P, P]), rhs=bg[:], start=True, stop=True)
        nc.scalar.copy(gain[:], gacc[:, 0:HD])
        def spread_bias(blk):
            bacc = psum.tile([P, BLOCK], F32, name="acc")
            for h in range(HEADS_BLOCK):
                k = HEADS_BLOCK * blk + h
                nc.tensor.matmul(
                    bacc[:, HD * h : HD * (h + 1)],
                    lhsT=ident[:, k : k + 1].to_broadcast([P, P]),
                    rhs=bg[:],
                    start=True,
                    stop=True,
                )
            nc.scalar.copy(bias[:, blk, :], bacc[:])

        for blk in range(HEAD_BLOCKS):
            spread_bias(blk)

        def build_table(i):
            pairs = fr[i][:].rearrange("p t (j k) -> p t j k", k=4)
            gains = gain[:].rearrange("p (j i) -> p j i", i=2)
            shape = [P, HALF_T, PAIRS, 2]
            for c, entries, gg in ((0, pairs[:, :, :, 0:4:3], gains), (1, pairs[:, :, :, 1:3], gains[:, :, ::-1])):
                nc.vector.tensor_tensor(
                    out=tab[i][:, c, :, :].rearrange("p t (j i) -> p t j i", i=2),
                    in0=entries,
                    in1=gg.unsqueeze(1).to_broadcast(shape),
                    op=MULT,
                )

        def split_table(i):
            nc.vector.tensor_copy(out=hi[i][:], in_=tab[i][:])
            nc.vector.tensor_tensor(out=lo[i][:], in0=tab[i][:], in1=hi[i][:], op=mybir.AluOpType.subtract)

        ptab = [[None, None], [None, None]]

        def place_table(i):
            for c in range(2):
                bank = psum_tab.tile([P, BLOCK], F32, name="ptab%d" % (2 * i + c))
                nc.tensor.matmul(bank[:], lhsT=ident[:], rhs=hi[i][:, c, :, :].rearrange("p t d -> p (t d)"), start=True, stop=False)
                nc.tensor.matmul(bank[:], lhsT=ident[:], rhs=lo[i][:, c, :, :].rearrange("p t d -> p (t d)"), start=False, stop=True)
                ptab[i][c] = bank

        for i in range(2):
            build_table(i)
            split_table(i)

        def mx_pass(acc, t, blk, k):
            i, tt = divmod(t, HALF_T)
            r = max(j for j in range(len(W_RANGES)) if W_RANGES[j][0] <= BLOCK * blk)
            c0 = BLOCK * blk - W_RANGES[r][0]
            nc.tensor.matmul_mx(
                out=acc[:],
                lhsT=xc[i][:, k, 2 * P * tt : 2 * P * (tt + 1)].bitcast(FP4X4),
                lhsT_scale=xs[i][:, k, P * tt : P * (tt + 1)],
                rhs=wc[r][:, k, 2 * c0 : 2 * (c0 + BLOCK)].bitcast(FP4X4),
                rhs_scale=ws[r][:, k, c0 : c0 + BLOCK],
                start=(k == 0),
                stop=(k == GROUPS - 1),
            )

        def part(tile, tiles):
            return tile[:, tiles[0] : tiles[1], :]

        def new_accs(n):
            accs = []
            for i in range(n):
                acc = psum.tile([P, BLOCK], F32, name="acc")
                accs.append(acc)
            return accs

        def multiply(unit):
            blk, t0, n = unit
            accs = new_accs(n)
            for i in range(n):
                for k in range(GROUPS):
                    mx_pass(accs[i], t0 + i, blk, k)
            return accs

        def multiply_first():
            accs = new_accs(4)
            for k in range(GROUPS // 2):
                for t in range(4):
                    mx_pass(accs[t], t, 0, k)
            place_table(0)
            for t in range(4):
                for k in range(GROUPS // 2, GROUPS):
                    mx_pass(accs[t], t, 0, k)
            return accs

        def add(engine, st, tiles):
            if tiles[1] > tiles[0]:
                engine.tensor_tensor(out=part(st["s0"], tiles), in0=part(st["s0"], tiles), in1=part(st["s1"], tiles), op=ADD)

        def product(dst, c, u, unit, tiles):
            blk, t0, n = unit
            i, tt = divmod(t0 + tiles[0], HALF_T)
            m = tiles[1] - tiles[0]
            shape = [P, m, HEADS_BLOCK, PAIRS, 2]
            channels = part(u, tiles).rearrange("p m (h j i) -> p m h j i", j=PAIRS, i=2)
            nc.vector.tensor_tensor(
                out=part(dst, tiles).rearrange("p m (h j i) -> p m h j i", j=PAIRS, i=2),
                in0=channels if c == 0 else channels[:, :, :, :, ::-1],
                in1=ptab[i][c][:, HD * tt : HD * (tt + m)]
                .rearrange("p (m j i) -> p m j i", j=PAIRS, i=2)
                .unsqueeze(2)
                .to_broadcast(shape),
                op=MULT,
            )

        def finish(st, tiles):
            blk, t0, n = st["unit"]
            for i in range(tiles[0], tiles[1]):
                for h in range(HEADS_BLOCK):
                    k = HEADS_BLOCK * i + h
                    nc.scalar.activation(
                        out=st["s0"][:, i, HD * h : HD * (h + 1)],
                        in_=st["s0"][:, i, HD * h : HD * (h + 1)],
                        func=ACT.Copy,
                        scale=st["rs"][:, k : k + 1],
                    )
            if tiles[1] > tiles[0]:
                nc.sync.dma_start(
                    out=out_v[:, t0 + tiles[0] : t0 + tiles[1], BLOCK * blk : BLOCK * (blk + 1)],
                    in_=part(st["s0"], tiles),
                )

        prev = None
        for q, unit in enumerate(UNITS):
            blk, t0, n = unit
            if q == 0:
                first = multiply_first()
                place_table(1)
            accs = first[2 * q : 2 * q + 2] if q < 2 else multiply(unit)
            u = work.tile([P, 2, BLOCK], F32, name="u", bufs=3)
            s0 = work.tile([P, 2, BLOCK], F32, name="s0", bufs=5)
            s1 = work.tile([P, 2, BLOCK], F32, name="s1", bufs=3)
            ss = small.tile([P, 8], F32, name="ss")
            rs = small.tile([P, 8], F32, name="rs")
            row = bias[:, blk, :] if blk < HEAD_BLOCKS else bias_late[:, blk - HEAD_BLOCKS, :]
            for i in range(n):
                nc.vector.tensor_tensor(out=u[:, i, :], in0=row, in1=accs[i][:], op=ADD)
            for i in range(n):
                for h in range(HEADS_BLOCK):
                    k = HEADS_BLOCK * i + h
                    junk = small.tile([P, HD], F32, name="junk", bufs=4)
                    nc.scalar.activation(
                        out=junk[:], in_=u[:, i, HD * h : HD * (h + 1)], func=ACT.Square, accum_out=ss[:, k : k + 1]
                    )
            nh = HEADS_BLOCK * n
            nc.scalar.activation(out=rs[:, 0:nh], in_=ss[:, 0:nh], func=ACT.Abs_reciprocal_sqrt, scale=1.0 / HD, bias=EPS)
            if q == 1:
                load_range(2)
            if q == 5:
                nc.sync.dma_start(
                    out=bias_late[:].rearrange("p c n -> p (c n)"), in_=b[BLOCK * HEAD_BLOCKS : C].partition_broadcast(P)
                )
            if q in (8, 16):
                load_range(3 if q == 8 else 4)
            if prev is not None:
                finish(prev, (0, prev["unit"][2]))
            for i in range(n):
                product(s0, 0, u, unit, (i, i + 1))
            product(s1, 1, u, unit, (0, n))
            prev = {"unit": unit, "s0": s0, "s1": s1, "rs": rs}
            if q < len(UNITS) - 1:
                add(nc.gpsimd, prev, (0, n))
        blk, t0, n = prev["unit"]
        for c0 in (0, 2 * HD):
            cols = slice(c0, c0 + 2 * HD)
            nc.vector.tensor_tensor(out=s0[:, 0, cols], in0=s0[:, 0, cols], in1=s1[:, 0, cols], op=ADD)
            for h in range(c0 // HD, c0 // HD + 2):
                hc = slice(HD * h, HD * (h + 1))
                nc.scalar.activation(out=s0[:, 0, hc], in_=s0[:, 0, hc], func=ACT.Copy, scale=rs[:, h : h + 1])
            nc.sync.dma_start(out=out_v[:, t0, BLOCK * blk + c0 : BLOCK * blk + c0 + 2 * HD], in_=s0[:, 0, cols])
